import numpy as np
import ml_dtypes


def mxq(x, axis, fmt="e4m3"):
    dtype, down = {"e4m3": (ml_dtypes.float8_e4m3fn, 7), "e5m2": (ml_dtypes.float8_e5m2, 14)}[fmt]
    v = np.moveaxis(np.asarray(x, np.float32).astype(ml_dtypes.bfloat16).astype(np.float64), axis, -1)
    blocks = v.reshape(v.shape[:-1] + (-1, 32))
    amax = np.abs(blocks).max(-1, keepdims=True)
    byte = np.maximum(np.where(amax > 0, np.frexp(amax)[1] - 1 + 127, 0) - down, 1)
    scale = np.exp2(byte - 127.0)
    codes = (blocks / scale).astype(np.float32).astype(dtype).astype(np.float64)
    return np.moveaxis((codes * scale).reshape(v.shape), -1, axis)


WIDE = False


def mx_kscale(k):
    if not WIDE:
        return np.ones(k)
    levels = np.array([10, -10, 5, -5, 0])
    a = np.random.permutation(np.resize(levels, k // 512 * 4)).reshape(k // 512, 4)
    idx = np.arange(k)
    return np.exp2(a[idx // 512, idx % 128 // 32])


BF16 = ml_dtypes.bfloat16


def bf(x):
    return np.asarray(x, np.float32).astype(BF16)


def f64(x):
    return np.asarray(x).astype(np.float64)


B, In, H, Hh, E, G = 512, 1024, 1024, 256, 128, 4
K = In + H
EPS = 1e-6


def rn(*shape):
    return np.random.standard_normal(shape)


def sigmoid(v):
    return 1.0 / (1.0 + np.exp(-v))


def ln(a, gamma, beta):
    mean = a.mean(-1, keepdims=True)
    std = a.std(-1, keepdims=True, ddof=1)
    return gamma * (a - mean) / (std + EPS) + beta


def setup_inputs():
    s = mx_kscale(K)
    return {
        'x': bf(rn(B, In) * s[:In]),
        'h': bf(rn(B, H) * s[In:]),
        'hyper_h': bf(rn(B, Hh)),
        'hyper_c': bf(rn(B, Hh)),
        'hc_Wih': bf(rn(G * Hh, K) / np.sqrt(K) / s[None, :]),
        'hc_bih': bf(0.3 * rn(G * Hh)),
        'hc_Whh': bf(rn(G * Hh, Hh) / np.sqrt(Hh)),
        'hc_ln_gamma': bf(1.0 + 0.1 * rn(G, Hh)),
        'hc_ln_beta': bf(0.1 * rn(G, Hh)),
        'hc_lnc_gamma': bf(1.0 + 0.1 * rn(Hh)),
        'hc_lnc_beta': bf(0.1 * rn(Hh)),
    }


def reference(x, h, hyper_h, hyper_c, hc_Wih, hc_bih, hc_Whh, hc_ln_gamma, hc_ln_beta, hc_lnc_gamma, hc_lnc_beta):
    hyper_in = np.concatenate([f64(x), f64(h)], axis=1)
    v = (mxq(hyper_in, 1, 'e4m3') @ mxq(f64(hc_Wih).T, 0, 'e4m3')) + f64(hc_bih) + f64(hyper_h) @ f64(hc_Whh).T
    v = ln(v.reshape(B, G, Hh), f64(hc_ln_gamma), f64(hc_ln_beta))
    hi, hf, hg, ho = v[:, 0], v[:, 1], v[:, 2], v[:, 3]
    hf = hf + 1.0
    new_hyper_c = f64(hyper_c) * sigmoid(hf) + sigmoid(hi) * np.tanh(hg)
    new_hyper_c = ln(new_hyper_c, f64(hc_lnc_gamma), f64(hc_lnc_beta))
    new_hyper_h = np.tanh(new_hyper_c) * sigmoid(ho)
    return new_hyper_h, new_hyper_c

@@ -1,0 +1,344 @@
+import math
+from contextlib import ExitStack
+
+import concourse.mybir as mybir
+from concourse.masks import make_identity
+
+F32 = mybir.dt.float32
+BF16 = mybir.dt.bfloat16
+U32 = mybir.dt.uint32
+U8 = mybir.dt.uint8
+FP8X4 = mybir.dt.float8_e4m3fn_x4
+ALU = mybir.AluOpType
+ACT = mybir.ActivationFunctionType
+
+P = 128
+BATCH = 512
+BT = BATCH // P
+IN = 1024
+K = 2 * IN
+UNITS = 256
+GATES = 4
+N = GATES * UNITS
+KH = UNITS // P
+K_PASS = 4 * P
+PASSES = K // K_PASS
+PASS_WORDS = K_PASS // 2
+BANK = 512
+EPS = 1e-6
+
+FLOPS = 2 * BATCH * N * K + 2 * BATCH * N * UNITS
+
+
+def tile_hyperlstmcell_pa_kernel(
+    tc,
+    x,
+    h,
+    hyper_h,
+    hyper_c,
+    hc_Wih,
+    hc_bih,
+    hc_Whh,
+    hc_ln_gamma,
+    hc_ln_beta,
+    hc_lnc_gamma,
+    hc_lnc_beta,
+    out_0,
+    out_1,
+):
+    nc = tc.nc
+    with ExitStack() as stack:
+        consts = stack.enter_context(tc.tile_pool(name="consts", bufs=1))
+        raw = stack.enter_context(tc.tile_pool(name="raw", bufs=1))
+        operands = stack.enter_context(tc.tile_pool(name="operands", bufs=1))
+        stage = stack.enter_context(tc.tile_pool(name="stage", bufs=3))
+        work = stack.enter_context(tc.tile_pool(name="work", bufs=2))
+        small = stack.enter_context(tc.tile_pool(name="small", bufs=2))
+        keep = stack.enter_context(tc.tile_pool(name="keep", bufs=1))
+        flip = stack.enter_context(tc.psum_pool(name="flip", bufs=4))
+        sums_psum = stack.enter_context(tc.psum_pool(name="sums_psum", bufs=4))
+
+        def block(t):
+            return slice(t * UNITS, (t + 1) * UNITS)
+
+        ident_f32 = consts.tile([P, P], F32)
+        make_identity(nc, ident_f32[:])
+        ident_bf16 = consts.tile([P, P], BF16)
+        make_identity(nc, ident_bf16[:])
+        ones = consts.tile([P, P], BF16)
+        nc.vector.memset(ones[:], 1.0)
+        half_power = consts.tile([P, BT], F32)
+        nc.vector.memset(half_power[:], 0.5)
+        one_column = consts.tile([P, 1], F32)
+        nc.vector.memset(one_column[:], 1.0)
+        table_warmer = consts.tile([P, 1], F32)
+        nc.scalar.activation(out=table_warmer[:], in_=one_column[:], func=ACT.Sigmoid)
+
+        bias_row = consts.tile([P, N], BF16)
+        nc.vector.memset(bias_row[:], 0.0)
+        nc.scalar.dma_start(out=bias_row[0:1, :], in_=hc_bih.rearrange("(o n) -> o n", o=1))
+        norm_rows = consts.tile([P, P], BF16)
+        nc.vector.memset(norm_rows[:], 0.0)
+        nc.scalar.dma_start(out=norm_rows[0:8, :], in_=hc_ln_gamma.rearrange("g (c q) -> (g c) q", q=P))
+        nc.scalar.dma_start(out=norm_rows[8:16, :], in_=hc_ln_beta.rearrange("g (c q) -> (g c) q", q=P))
+        nc.scalar.dma_start(out=norm_rows[16:18, :], in_=hc_lnc_gamma.rearrange("(c q) -> c q", q=P))
+        nc.scalar.dma_start(out=norm_rows[18:20, :], in_=hc_lnc_beta.rearrange("(c q) -> c q", q=P))
+        NORM_CHUNKS = 20
+
+        hh_raw = raw.tile([P, BT * UNITS], BF16)
+        nc.sync.dma_start(out=hh_raw[:], in_=hyper_h.rearrange("(p t) k -> p (t k)", t=BT))
+        whh_raw = raw.tile([P, (N // P) * UNITS], BF16)
+        nc.sync.dma_start(
+            out=whh_raw[:].rearrange("p (j k) -> p j k", k=UNITS),
+            in_=hc_Whh.rearrange("(j p) k -> p j k", p=P),
+        )
+        x_raw = raw.tile([P, BT * IN], BF16)
+        nc.sync.dma_start(out=x_raw[:], in_=x.rearrange("(p t) k -> p (t k)", t=BT))
+        h_raw = raw.tile([P, BT * IN], BF16)
+        nc.sync.dma_start(out=h_raw[:], in_=h.rearrange("(p t) k -> p (t k)", t=BT))
+        c_raw = raw.tile([P, BT * UNITS], BF16)
+        w_raw = []
+        for gate in range(GATES):
+            w_gate = raw.tile([P, 2 * K], BF16, name="w_raw%d" % gate)
+            nc.sync.dma_start(
+                out=w_gate[:].rearrange("p (j k) -> p j k", k=K),
+                in_=hc_Wih[gate * UNITS : (gate + 1) * UNITS, :].rearrange("(j p) k -> p j k", p=P),
+            )
+            w_raw.append(w_gate)
+            if gate == 1:
+                nc.sync.dma_start(out=c_raw[:], in_=hyper_c.rearrange("(p t) n -> p (t n)", t=BT))
+
+        norm_cols_psum = flip.tile([P, 2 * BANK], BF16, tag="flip")
+        nc.tensor.transpose(out=norm_cols_psum[:, 0:P], in_=norm_rows[:], identity=ident_bf16[:])
+        norm_cols = consts.tile([P, P], BF16)
+        nc.vector.tensor_copy(out=norm_cols[:], in_=norm_cols_psum[:, 0:P])
+        norm_all = consts.tile([P, NORM_CHUNKS * P], BF16)
+        CHUNKS_PER_BANK = 2 * BANK // P
+        for first in range(0, NORM_CHUNKS, CHUNKS_PER_BANK):
+            chunks = min(CHUNKS_PER_BANK, NORM_CHUNKS - first)
+            spread = flip.tile([P, 2 * BANK], BF16, tag="flip")
+            for i in range(chunks):
+                nc.tensor.transpose(
+                    out=spread[:, i * P : (i + 1) * P],
+                    in_=norm_cols[:, first + i : first + i + 1].to_broadcast([P, P]),
+                    identity=ident_bf16[:],
+                )
+            nc.vector.tensor_copy(
+                out=norm_all[:, first * P : (first + chunks) * P], in_=spread[:, 0 : chunks * P]
+            )
+        ln_gamma = norm_all[:, 0:N]
+        ln_beta = norm_all[:, N : 2 * N]
+        lnc_gamma = norm_all[:, 2 * N : 2 * N + UNITS]
+        lnc_beta = norm_all[:, 2 * N + UNITS : 2 * N + 2 * UNITS]
+
+        hh_t = operands.tile([P, KH * BT * P], BF16)
+        hh_t_psum = flip.tile([P, 2 * BANK], BF16, tag="flip")
+        for step in range(KH):
+            for t in range(BT):
+                nc.tensor.transpose(
+                    out=hh_t_psum[:, (step * BT + t) * P : (step * BT + t + 1) * P],
+                    in_=hh_raw[:, t * UNITS + step * P : t * UNITS + (step + 1) * P],
+                    identity=ident_bf16[:],
+                )
+        nc.vector.tensor_copy(out=hh_t[:], in_=hh_t_psum[:])
+        whh_t = operands.tile([P, KH * N], BF16)
+        for step in range(KH):
+            whh_t_psum = flip.tile([P, 2 * BANK], BF16, tag="flip")
+            for j in range(N // P):
+                nc.tensor.transpose(
+                    out=whh_t_psum[:, j * P : (j + 1) * P],
+                    in_=whh_raw[:, j * UNITS + step * P : j * UNITS + (step + 1) * P],
+                    identity=ident_bf16[:],
+                )
+            nc.vector.tensor_copy(out=whh_t[:, step * N : (step + 1) * N], in_=whh_t_psum[:])
+
+        plain = operands.tile([P, BT * N], F32)
+        for n0 in range(0, N, BANK):
+            for t in range(BT):
+                plain_psum = sums_psum.tile([P, BANK], F32, tag="sums")
+                for step in range(KH):
+                    nc.tensor.matmul(
+                        out=plain_psum[:],
+                        lhsT=hh_t[:, (step * BT + t) * P : (step * BT + t + 1) * P],
+                        rhs=whh_t[:, step * N + n0 : step * N + n0 + BANK],
+                        start=(step == 0),
+                        stop=False,
+                    )
+                nc.tensor.matmul(
+                    out=plain_psum[:], lhsT=ones[:], rhs=bias_row[:, n0 : n0 + BANK], start=False, stop=True
+                )
+                nc.scalar.copy(out=plain[:, t * N + n0 : t * N + n0 + BANK], in_=plain_psum[:])
+
+        u_codes = operands.tile([P, PASSES * BATCH], U32, align_bytes=64)
+        u_scales = operands.tile([P, PASSES * BATCH], U8, align_bytes=64)
+        w_codes = operands.tile([P, GATES * PASSES * UNITS], U32, align_bytes=64)
+        w_scales = operands.tile([P, GATES * PASSES * UNITS], U8, align_bytes=64)
+
+        def quantise(pieces, codes, scales, vector_helps):
+            grouped = stage.tile([P, 2 * BANK * 2], BF16, align_bytes=64)
+            grouped_words = grouped[:].bitcast(F32)
+            for b in range(2):
+                row_tiles, first_word = pieces[b]
+                bank = flip.tile([P, BANK], F32, tag="flip")
+                for half in range(2):
+                    for i in range(2):
+                        nc.tensor.transpose(
+                            out=bank[:, (2 * half + i) * P : (2 * half + i + 1) * P],
+                            in_=row_tiles[i][:, first_word + half * P : first_word + (half + 1) * P],
+                            identity=ident_f32[:],
+                        )
+                side_by_side = grouped_words[:, b * BANK : (b + 1) * BANK].rearrange("p (r u) -> p r u", u=2)
+                halves = bank[:].rearrange("p (u r) -> p r u", u=2)
+                if vector_helps and b == 0:
+                    nc.vector.tensor_copy(out=side_by_side, in_=halves)
+                else:
+                    nc.scalar.copy(out=side_by_side, in_=halves)
+            nc.vector.quantize_mx(out=codes.bitcast(FP8X4), scales=scales, in_=grouped[:])
+
+        def quantise_u(g):
+            source = (x_raw if g < PASSES // 2 else h_raw)[:].bitcast(F32)
+            row_words = IN // 2
+            first_word = (g % (PASSES // 2)) * PASS_WORDS
+            tiles = [source[:, t * row_words : (t + 1) * row_words] for t in range(BT)]
+            quantise(
+                [(tiles[0:2], first_word), (tiles[2:4], first_word)],
+                u_codes[:, g * BATCH : (g + 1) * BATCH],
+                u_scales[:, g * BATCH : (g + 1) * BATCH],
+                vector_helps=True,
+            )
+
+        def quantise_w(gate):
+            source = w_raw[gate][:].bitcast(F32)
+            row_words = K // 2
+            tiles = [source[:, j * row_words : (j + 1) * row_words] for j in range(2)]
+            for g in range(0, PASSES, 2):
+                first = (gate * PASSES + g) * UNITS
+                quantise(
+                    [(tiles, g * PASS_WORDS), (tiles, (g + 1) * PASS_WORDS)],
+                    w_codes[:, first : first + 2 * UNITS],
+                    w_scales[:, first : first + 2 * UNITS],
+                    vector_helps=(gate == 0),
+                )
+
+        def layer_norm(values, sums, gamma, beta, out):
+            shrink = 1.0 / math.sqrt(UNITS - 1)
+            neg_mean = small.tile([P, BT], F32, tag="neg_mean")
+            nc.vector.tensor_scalar_mul(out=neg_mean[:], in0=sums, scalar1=-1.0 / UNITS)
+            neg_mean_shrunk = small.tile([P, BT], F32, tag="neg_mean_shrunk")
+            nc.vector.tensor_scalar_mul(out=neg_mean_shrunk[:], in0=sums, scalar1=-shrink / UNITS)
+            variance = small.tile([P, BT], F32, tag="variance")
+            squares = work.tile([P, BT * UNITS], F32, tag="squares")
+            for t in range(BT):
+                nc.scalar.activation(
+                    out=squares[:, block(t)],
+                    in_=values[:, block(t)],
+                    func=ACT.Square,
+                    bias=neg_mean_shrunk[:, t : t + 1],
+                    scale=shrink,
+                    accum_out=variance[:, t : t + 1],
+                )
+            std = small.tile([P, BT], F32, tag="std")
+            nc.gpsimd.tensor_tensor(out=std[:], in0=variance[:], in1=half_power[:], op=ALU.pow)
+            std_eps = small.tile([P, BT], F32, tag="std_eps")
+            nc.vector.tensor_scalar_add(out=std_eps[:], in0=std[:], scalar1=EPS)
+            inv_std = small.tile([P, BT], F32, tag="inv_std")
+            nc.vector.reciprocal(out=inv_std[:], in_=std_eps[:])
+            centred = work.tile([P, BT * UNITS], F32, tag="centred")
+            for t in range(BT):
+                nc.vector.scalar_tensor_tensor(
+                    out=centred[:, block(t)],
+                    in0=values[:, block(t)],
+                    scalar=neg_mean[:, t : t + 1],
+                    in1=gamma,
+                    op0=ALU.add,
+                    op1=ALU.mult,
+                )
+            for t in range(BT):
+                nc.vector.scalar_tensor_tensor(
+                    out=out[:, block(t)],
+                    in0=centred[:, block(t)],
+                    scalar=inv_std[:, t : t + 1],
+                    in1=beta,
+                    op0=ALU.mult,
+                    op1=ALU.add,
+                )
+
+        def gate_output(gate, func, bias):
+            v = work.tile([P, BT * UNITS], F32, tag="v")
+            v_sums = small.tile([P, BT], F32, tag="v_sums")
+            for pair in range(BT // 2):
+                mx_psum = sums_psum.tile([P, BANK], F32, tag="sums")
+                for i in range(2):
+                    t = 2 * pair + i
+                    for g in range(PASSES):
+                        u_cols = slice(g * BATCH + t * P, g * BATCH + (t + 1) * P)
+                        w_cols = slice((gate * PASSES + g) * UNITS, (gate * PASSES + g + 1) * UNITS)
+                        nc.tensor.matmul_mx(
+                            out=mx_psum[:, i * UNITS : (i + 1) * UNITS],
+                            lhsT=u_codes[:, u_cols].bitcast(FP8X4),
+                            lhsT_scale=u_scales[:, u_cols],
+                            rhs=w_codes[:, w_cols].bitcast(FP8X4),
+                            rhs_scale=w_scales[:, w_cols],
+                            start=(g == 0),
+                            stop=(g == PASSES - 1),
+                        )
+                for i in range(2):
+                    t = 2 * pair + i
+                    nc.vector.scalar_tensor_tensor(
+                        out=v[:, block(t)],
+                        in0=mx_psum[:, i * UNITS : (i + 1) * UNITS],
+                        scalar=1.0,
+                        in1=plain[:, t * N + gate * UNITS : t * N + (gate + 1) * UNITS],
+                        op0=ALU.mult,
+                        op1=ALU.add,
+                        accum_out=v_sums[:, t : t + 1],
+                    )
+            normed = work.tile([P, BT * UNITS], F32, tag="normed")
+            gate_cols = slice(gate * UNITS, (gate + 1) * UNITS)
+            layer_norm(v, v_sums[:], ln_gamma[:, gate_cols], ln_beta[:, gate_cols], normed)
+            result = keep.tile([P, BT * UNITS], F32, name="gate%d" % gate)
+            for t in range(BT):
+                if bias is None:
+                    nc.scalar.activation(out=result[:, block(t)], in_=normed[:, block(t)], func=func)
+                else:
+                    nc.scalar.activation(out=result[:, block(t)], in_=normed[:, block(t)], func=func, bias=bias)
+            return result
+
+        for g in range(PASSES):
+            quantise_u(g)
+        quantise_w(0)
+        quantise_w(1)
+        gate_i = gate_output(0, ACT.Sigmoid, None)
+        quantise_w(2)
+        gate_f = gate_output(1, ACT.Sigmoid, one_column[:])
+        kept = keep.tile([P, BT * UNITS], F32)
+        nc.vector.tensor_tensor(out=kept[:], in0=gate_f[:], in1=c_raw[:], op=ALU.mult)
+        quantise_w(3)
+        gate_g = gate_output(2, ACT.Tanh, None)
+        fresh = keep.tile([P, BT * UNITS], F32)
+        nc.vector.tensor_tensor(out=fresh[:], in0=gate_i[:], in1=gate_g[:], op=ALU.mult)
+        cell = keep.tile([P, BT * UNITS], F32)
+        cell_sums = small.tile([P, BT], F32)
+        for t in range(BT):
+            nc.vector.scalar_tensor_tensor(
+                out=cell[:, block(t)],
+                in0=kept[:, block(t)],
+                scalar=1.0,
+                in1=fresh[:, block(t)],
+                op0=ALU.mult,
+                op1=ALU.add,
+                accum_out=cell_sums[:, t : t + 1],
+            )
+        gate_o = gate_output(3, ACT.Sigmoid, None)
+        new_c = keep.tile([P, BT * UNITS], F32)
+        layer_norm(cell, cell_sums[:], lnc_gamma, lnc_beta, new_c)
+        nc.sync.dma_start(out=out_1.rearrange("(p t) n -> p (t n)", t=BT), in_=new_c[:])
+        tanh_c = keep.tile([P, BT * UNITS], F32)
+        new_h = keep.tile([P, BT * UNITS], F32)
+        out_0_tiles = out_0.rearrange("(p t) n -> p t n", t=BT)
+        for t in range(BT):
+            nc.scalar.activation(out=tanh_c[:, block(t)], in_=new_c[:, block(t)], func=ACT.Tanh)
+            nc.vector.tensor_tensor(
+                out=new_h[:, block(t)], in0=tanh_c[:, block(t)], in1=gate_o[:, block(t)], op=ALU.mult
+            )
+            nc.sync.dma_start(out=out_0_tiles[:, t, :], in_=new_h[:, block(t)])

@@ -48,43 +48,44 @@ def tile_hyperlstmcell_pa_kernel(
 ):
     nc = tc.nc
     with ExitStack() as stack:
+        stack.enter_context(tc.manual_schedule())
         consts = stack.enter_context(tc.tile_pool(name="consts", bufs=1))
         raw = stack.enter_context(tc.tile_pool(name="raw", bufs=1))
         operands = stack.enter_context(tc.tile_pool(name="operands", bufs=1))
-        stage = stack.enter_context(tc.tile_pool(name="stage", bufs=3))
+        stage = stack.enter_context(tc.tile_pool(name="stage", bufs=4))
         work = stack.enter_context(tc.tile_pool(name="work", bufs=2))
-        small = stack.enter_context(tc.tile_pool(name="small", bufs=2))
+        small = stack.enter_context(tc.tile_pool(name="small", bufs=3))
         keep = stack.enter_context(tc.tile_pool(name="keep", bufs=1))
-        flip = stack.enter_context(tc.psum_pool(name="flip", bufs=4))
-        sums_psum = stack.enter_context(tc.psum_pool(name="sums_psum", bufs=4))
+        flip_psum = stack.enter_context(tc.psum_pool(name="flip_psum", bufs=4))
+        mx_psum = stack.enter_context(tc.psum_pool(name="mx_psum", bufs=2))
+        plain_psum = stack.enter_context(tc.psum_pool(name="plain_psum", bufs=2))
 
         def block(t):
             return slice(t * UNITS, (t + 1) * UNITS)
 
-        ident_f32 = consts.tile([P, P], F32)
-        make_identity(nc, ident_f32[:])
-        ident_bf16 = consts.tile([P, P], BF16)
-        make_identity(nc, ident_bf16[:])
+        norm_rows = consts.tile([P, P], BF16)
+        nc.vector.memset(norm_rows[:], 0.0)
+        bias_row = consts.tile([P, N], BF16)
+        nc.vector.memset(bias_row[:], 0.0)
         ones = consts.tile([P, P], BF16)
         nc.vector.memset(ones[:], 1.0)
         half_power = consts.tile([P, BT], F32)
         nc.vector.memset(half_power[:], 0.5)
         one_column = consts.tile([P, 1], F32)
         nc.vector.memset(one_column[:], 1.0)
+        ident_bf16 = consts.tile([P, P], BF16)
+        make_identity(nc, ident_bf16[:])
+        ident_f32 = consts.tile([P, P], F32)
+        make_identity(nc, ident_f32[:])
         table_warmer = consts.tile([P, 1], F32)
         nc.scalar.activation(out=table_warmer[:], in_=one_column[:], func=ACT.Sigmoid)
 
-        bias_row = consts.tile([P, N], BF16)
-        nc.vector.memset(bias_row[:], 0.0)
-        nc.scalar.dma_start(out=bias_row[0:1, :], in_=hc_bih.rearrange("(o n) -> o n", o=1))
-        norm_rows = consts.tile([P, P], BF16)
-        nc.vector.memset(norm_rows[:], 0.0)
-        nc.scalar.dma_start(out=norm_rows[0:8, :], in_=hc_ln_gamma.rearrange("g (c q) -> (g c) q", q=P))
-        nc.scalar.dma_start(out=norm_rows[8:16, :], in_=hc_ln_beta.rearrange("g (c q) -> (g c) q", q=P))
-        nc.scalar.dma_start(out=norm_rows[16:18, :], in_=hc_lnc_gamma.rearrange("(c q) -> c q", q=P))
-        nc.scalar.dma_start(out=norm_rows[18:20, :], in_=hc_lnc_beta.rearrange("(c q) -> c q", q=P))
+        nc.sync.dma_start(out=norm_rows[0:8, :], in_=hc_ln_gamma.rearrange("g (c q) -> (g c) q", q=P))
+        nc.sync.dma_start(out=norm_rows[8:16, :], in_=hc_ln_beta.rearrange("g (c q) -> (g c) q", q=P))
+        nc.sync.dma_start(out=norm_rows[16:18, :], in_=hc_lnc_gamma.rearrange("(c q) -> c q", q=P))
+        nc.sync.dma_start(out=norm_rows[18:20, :], in_=hc_lnc_beta.rearrange("(c q) -> c q", q=P))
         NORM_CHUNKS = 20
-
+        nc.sync.dma_start(out=bias_row[0:1, :], in_=hc_bih.rearrange("(o n) -> o n", o=1))
         hh_raw = raw.tile([P, BT * UNITS], BF16)
         nc.sync.dma_start(out=hh_raw[:], in_=hyper_h.rearrange("(p t) k -> p (t k)", t=BT))
         whh_raw = raw.tile([P, (N // P) * UNITS], BF16)
@@ -108,7 +109,7 @@ def tile_hyperlstmcell_pa_kernel(
             if gate == 1:
                 nc.sync.dma_start(out=c_raw[:], in_=hyper_c.rearrange("(p t) n -> p (t n)", t=BT))
 
-        norm_cols_psum = flip.tile([P, 2 * BANK], BF16, tag="flip")
+        norm_cols_psum = flip_psum.tile([P, 2 * BANK], BF16, tag="flip")
         nc.tensor.transpose(out=norm_cols_psum[:, 0:P], in_=norm_rows[:], identity=ident_bf16[:])
         norm_cols = consts.tile([P, P], BF16)
         nc.vector.tensor_copy(out=norm_cols[:], in_=norm_cols_psum[:, 0:P])
@@ -116,7 +117,7 @@ def tile_hyperlstmcell_pa_kernel(
         CHUNKS_PER_BANK = 2 * BANK // P
         for first in range(0, NORM_CHUNKS, CHUNKS_PER_BANK):
             chunks = min(CHUNKS_PER_BANK, NORM_CHUNKS - first)
-            spread = flip.tile([P, 2 * BANK], BF16, tag="flip")
+            spread = flip_psum.tile([P, 2 * BANK], BF16, tag="flip")
             for i in range(chunks):
                 nc.tensor.transpose(
                     out=spread[:, i * P : (i + 1) * P],
@@ -132,7 +133,7 @@ def tile_hyperlstmcell_pa_kernel(
         lnc_beta = norm_all[:, 2 * N + UNITS : 2 * N + 2 * UNITS]
 
         hh_t = operands.tile([P, KH * BT * P], BF16)
-        hh_t_psum = flip.tile([P, 2 * BANK], BF16, tag="flip")
+        hh_t_psum = flip_psum.tile([P, 2 * BANK], BF16, tag="flip")
         for step in range(KH):
             for t in range(BT):
                 nc.tensor.transpose(
@@ -143,43 +144,50 @@ def tile_hyperlstmcell_pa_kernel(
         nc.vector.tensor_copy(out=hh_t[:], in_=hh_t_psum[:])
         whh_t = operands.tile([P, KH * N], BF16)
         for step in range(KH):
-            whh_t_psum = flip.tile([P, 2 * BANK], BF16, tag="flip")
+            whh_t_psum = flip_psum.tile([P, 2 * BANK], BF16, tag="flip")
             for j in range(N // P):
                 nc.tensor.transpose(
                     out=whh_t_psum[:, j * P : (j + 1) * P],
                     in_=whh_raw[:, j * UNITS + step * P : j * UNITS + (step + 1) * P],
                     identity=ident_bf16[:],
                 )
-            nc.vector.tensor_copy(out=whh_t[:, step * N : (step + 1) * N], in_=whh_t_psum[:])
+            if step == 0:
+                nc.vector.tensor_copy(out=whh_t[:, step * N : (step + 1) * N], in_=whh_t_psum[:])
+            else:
+                nc.scalar.copy(out=whh_t[:, step * N : (step + 1) * N], in_=whh_t_psum[:])
 
-        plain = operands.tile([P, BT * N], F32)
-        for n0 in range(0, N, BANK):
-            for t in range(BT):
-                plain_psum = sums_psum.tile([P, BANK], F32, tag="sums")
-                for step in range(KH):
-                    nc.tensor.matmul(
-                        out=plain_psum[:],
-                        lhsT=hh_t[:, (step * BT + t) * P : (step * BT + t + 1) * P],
-                        rhs=whh_t[:, step * N + n0 : step * N + n0 + BANK],
-                        start=(step == 0),
-                        stop=False,
-                    )
-                nc.tensor.matmul(
-                    out=plain_psum[:], lhsT=ones[:], rhs=bias_row[:, n0 : n0 + BANK], start=False, stop=True
-                )
-                nc.scalar.copy(out=plain[:, t * N + n0 : t * N + n0 + BANK], in_=plain_psum[:])
+        plain = operands.tile([P, GATES * BT * UNITS], F32)
+
+        def plain_product(gate):
+            units = slice(gate * UNITS, (gate + 1) * UNITS)
+            for pair in range(BT // 2):
+                bank = plain_psum.tile([P, BANK], F32, tag="plain")
+                for i in range(2):
+                    t = 2 * pair + i
+                    group = bank[:, i * UNITS : (i + 1) * UNITS]
+                    for step in range(KH):
+                        nc.tensor.matmul(
+                            out=group,
+                            lhsT=hh_t[:, (step * BT + t) * P : (step * BT + t + 1) * P],
+                            rhs=whh_t[:, step * N + gate * UNITS : step * N + (gate + 1) * UNITS],
+                            start=(step == 0),
+                            stop=False,
+                        )
+                    nc.tensor.matmul(out=group, lhsT=ones[:], rhs=bias_row[:, units], start=False, stop=True)
+                first = (gate * BT + 2 * pair) * UNITS
+                nc.scalar.copy(out=plain[:, first : first + BANK], in_=bank[:])
 
         u_codes = operands.tile([P, PASSES * BATCH], U32, align_bytes=64)
         u_scales = operands.tile([P, PASSES * BATCH], U8, align_bytes=64)
         w_codes = operands.tile([P, GATES * PASSES * UNITS], U32, align_bytes=64)
         w_scales = operands.tile([P, GATES * PASSES * UNITS], U8, align_bytes=64)
 
-        def quantise(pieces, codes, scales, vector_helps):
-            grouped = stage.tile([P, 2 * BANK * 2], BF16, align_bytes=64)
+        def flip(pieces, vector_helps):
+            grouped = stage.tile([P, 2 * BANK * 2], BF16, align_bytes=64, tag="grouped")
             grouped_words = grouped[:].bitcast(F32)
             for b in range(2):
                 row_tiles, first_word = pieces[b]
-                bank = flip.tile([P, BANK], F32, tag="flip")
+                bank = flip_psum.tile([P, BANK], F32, tag="flip")
                 for half in range(2):
                     for i in range(2):
                         nc.tensor.transpose(
@@ -193,56 +201,49 @@ def tile_hyperlstmcell_pa_kernel(
                     nc.vector.tensor_copy(out=side_by_side, in_=halves)
                 else:
                     nc.scalar.copy(out=side_by_side, in_=halves)
-            nc.vector.quantize_mx(out=codes.bitcast(FP8X4), scales=scales, in_=grouped[:])
+            return grouped
 
-        def quantise_u(g):
+        def flip_u(g):
             source = (x_raw if g < PASSES // 2 else h_raw)[:].bitcast(F32)
             row_words = IN // 2
             first_word = (g % (PASSES // 2)) * PASS_WORDS
             tiles = [source[:, t * row_words : (t + 1) * row_words] for t in range(BT)]
-            quantise(
-                [(tiles[0:2], first_word), (tiles[2:4], first_word)],
-                u_codes[:, g * BATCH : (g + 1) * BATCH],
-                u_scales[:, g * BATCH : (g + 1) * BATCH],
-                vector_helps=True,
-            )
+            return flip([(tiles[0:2], first_word), (tiles[2:4], first_word)], vector_helps=True)
 
-        def quantise_w(gate):
+        def quantise_u(g, grouped):
+            cols = slice(g * BATCH, (g + 1) * BATCH)
+            nc.vector.quantize_mx(out=u_codes[:, cols].bitcast(FP8X4), scales=u_scales[:, cols], in_=grouped[:])
+
+        def flip_w(gate, vector_helps):
             source = w_raw[gate][:].bitcast(F32)
             row_words = K // 2
             tiles = [source[:, j * row_words : (j + 1) * row_words] for j in range(2)]
-            for g in range(0, PASSES, 2):
-                first = (gate * PASSES + g) * UNITS
-                quantise(
-                    [(tiles, g * PASS_WORDS), (tiles, (g + 1) * PASS_WORDS)],
-                    w_codes[:, first : first + 2 * UNITS],
-                    w_scales[:, first : first + 2 * UNITS],
-                    vector_helps=(gate == 0),
+            return [
+                flip([(tiles, g * PASS_WORDS), (tiles, (g + 1) * PASS_WORDS)], vector_helps)
+                for g in range(0, PASSES, 2)
+            ]
+
+        def quantise_w(gate, grouped_pair):
+            for i in range(2):
+                first = (gate * PASSES + 2 * i) * UNITS
+                cols = slice(first, first + 2 * UNITS)
+                nc.vector.quantize_mx(
+                    out=w_codes[:, cols].bitcast(FP8X4), scales=w_scales[:, cols], in_=grouped_pair[i][:]
                 )
 
-        def layer_norm(values, sums, gamma, beta, out):
-            shrink = 1.0 / math.sqrt(UNITS - 1)
+        def start_norm(values, sums, gamma):
             neg_mean = small.tile([P, BT], F32, tag="neg_mean")
-            nc.vector.tensor_scalar_mul(out=neg_mean[:], in0=sums, scalar1=-1.0 / UNITS)
-            neg_mean_shrunk = small.tile([P, BT], F32, tag="neg_mean_shrunk")
-            nc.vector.tensor_scalar_mul(out=neg_mean_shrunk[:], in0=sums, scalar1=-shrink / UNITS)
-            variance = small.tile([P, BT], F32, tag="variance")
+            nc.vector.tensor_scalar_mul(out=neg_mean[:], in0=sums[:], scalar1=-1.0 / UNITS)
+            sum_squares = small.tile([P, BT], F32, tag="sum_squares")
             squares = work.tile([P, BT * UNITS], F32, tag="squares")
             for t in range(BT):
                 nc.scalar.activation(
                     out=squares[:, block(t)],
                     in_=values[:, block(t)],
                     func=ACT.Square,
-                    bias=neg_mean_shrunk[:, t : t + 1],
-                    scale=shrink,
-                    accum_out=variance[:, t : t + 1],
+                    bias=neg_mean[:, t : t + 1],
+                    accum_out=sum_squares[:, t : t + 1],
                 )
-            std = small.tile([P, BT], F32, tag="std")
-            nc.gpsimd.tensor_tensor(out=std[:], in0=variance[:], in1=half_power[:], op=ALU.pow)
-            std_eps = small.tile([P, BT], F32, tag="std_eps")
-            nc.vector.tensor_scalar_add(out=std_eps[:], in0=std[:], scalar1=EPS)
-            inv_std = small.tile([P, BT], F32, tag="inv_std")
-            nc.vector.reciprocal(out=inv_std[:], in_=std_eps[:])
             centred = work.tile([P, BT * UNITS], F32, tag="centred")
             for t in range(BT):
                 nc.vector.scalar_tensor_tensor(
@@ -253,6 +254,22 @@ def tile_hyperlstmcell_pa_kernel(
                     op0=ALU.add,
                     op1=ALU.mult,
                 )
+            root = small.tile([P, BT], F32, tag="root")
+            nc.gpsimd.tensor_tensor(out=root[:], in0=sum_squares[:], in1=half_power[:], op=ALU.pow)
+            return centred, root
+
+        def finish_norm(centred, root, beta, out):
+            std_eps = small.tile([P, BT], F32, tag="std_eps")
+            nc.vector.tensor_scalar(
+                out=std_eps[:],
+                in0=root[:],
+                scalar1=1.0 / math.sqrt(UNITS - 1),
+                scalar2=EPS,
+                op0=ALU.mult,
+                op1=ALU.add,
+            )
+            inv_std = small.tile([P, BT], F32, tag="inv_std")
+            nc.vector.reciprocal(out=inv_std[:], in_=std_eps[:])
             for t in range(BT):
                 nc.vector.scalar_tensor_tensor(
                     out=out[:, block(t)],
@@ -263,18 +280,18 @@ def tile_hyperlstmcell_pa_kernel(
                     op1=ALU.add,
                 )
 
-        def gate_output(gate, func, bias):
+        def gate_sums(gate):
             v = work.tile([P, BT * UNITS], F32, tag="v")
             v_sums = small.tile([P, BT], F32, tag="v_sums")
             for pair in range(BT // 2):
-                mx_psum = sums_psum.tile([P, BANK], F32, tag="sums")
+                bank = mx_psum.tile([P, BANK], F32, tag="mx")
                 for i in range(2):
                     t = 2 * pair + i
                     for g in range(PASSES):
                         u_cols = slice(g * BATCH + t * P, g * BATCH + (t + 1) * P)
                         w_cols = slice((gate * PASSES + g) * UNITS, (gate * PASSES + g + 1) * UNITS)
                         nc.tensor.matmul_mx(
-                            out=mx_psum[:, i * UNITS : (i + 1) * UNITS],
+                            out=bank[:, i * UNITS : (i + 1) * UNITS],
                             lhsT=u_codes[:, u_cols].bitcast(FP8X4),
                             lhsT_scale=u_scales[:, u_cols],
                             rhs=w_codes[:, w_cols].bitcast(FP8X4),
@@ -286,37 +303,62 @@ def tile_hyperlstmcell_pa_kernel(
                     t = 2 * pair + i
                     nc.vector.scalar_tensor_tensor(
                         out=v[:, block(t)],
-                        in0=mx_psum[:, i * UNITS : (i + 1) * UNITS],
+                        in0=bank[:, i * UNITS : (i + 1) * UNITS],
                         scalar=1.0,
-                        in1=plain[:, t * N + gate * UNITS : t * N + (gate + 1) * UNITS],
+                        in1=plain[:, (gate * BT + t) * UNITS : (gate * BT + t + 1) * UNITS],
                         op0=ALU.mult,
                         op1=ALU.add,
                         accum_out=v_sums[:, t : t + 1],
                     )
-            normed = work.tile([P, BT * UNITS], F32, tag="normed")
-            gate_cols = slice(gate * UNITS, (gate + 1) * UNITS)
-            layer_norm(v, v_sums[:], ln_gamma[:, gate_cols], ln_beta[:, gate_cols], normed)
-            result = keep.tile([P, BT * UNITS], F32, name="gate%d" % gate)
-            for t in range(BT):
-                if bias is None:
-                    nc.scalar.activation(out=result[:, block(t)], in_=normed[:, block(t)], func=func)
-                else:
-                    nc.scalar.activation(out=result[:, block(t)], in_=normed[:, block(t)], func=func, bias=bias)
-            return result
+            return v, v_sums
 
-        for g in range(PASSES):
-            quantise_u(g)
-        quantise_w(0)
-        quantise_w(1)
-        gate_i = gate_output(0, ACT.Sigmoid, None)
-        quantise_w(2)
-        gate_f = gate_output(1, ACT.Sigmoid, one_column[:])
+        def gate_cols(gate):
+            return slice(gate * UNITS, (gate + 1) * UNITS)
+
+        GATE_FUNC = [ACT.Sigmoid, ACT.Sigmoid, ACT.Tanh, ACT.Sigmoid]
+        gates = [keep.tile([P, BT * UNITS], F32, name="gate%d" % gate) for gate in range(GATES)]
+
+        def activate(gate, normed, tiles_at_once):
+            width = tiles_at_once * UNITS
+            for first in range(0, BT * UNITS, width):
+                cols = slice(first, first + width)
+                if gate == 1:
+                    nc.scalar.activation(
+                        out=gates[gate][:, cols], in_=normed[:, cols], func=GATE_FUNC[gate], bias=one_column[:]
+                    )
+                else:
+                    nc.scalar.activation(out=gates[gate][:, cols], in_=normed[:, cols], func=GATE_FUNC[gate])
+
+        grouped_u = [flip_u(0), flip_u(1)]
+        quantise_u(0, grouped_u[0])
+        plain_product(0)
+        quantise_u(1, grouped_u[1])
+        grouped_u = grouped_u + [flip_u(2), flip_u(3)]
+        quantise_u(2, grouped_u[2])
+        quantise_u(3, grouped_u[3])
+        quantise_w(0, flip_w(0, vector_helps=True))
+        quantise_w(1, flip_w(1, vector_helps=False))
+
+        started = []
+        for gate in range(GATES):
+            v, v_sums = gate_sums(gate)
+            started.append(start_norm(v, v_sums, ln_gamma[:, gate_cols(gate)]))
+            if gate >= 1:
+                normed = work.tile([P, BT * UNITS], F32, tag="normed")
+                finish_norm(started[gate - 1][0], started[gate - 1][1], ln_beta[:, gate_cols(gate - 1)], normed)
+            if gate + 2 < GATES:
+                grouped_w = flip_w(gate + 2, vector_helps=False)
+            if gate + 1 < GATES:
+                plain_product(gate + 1)
+            if gate + 2 < GATES:
+                quantise_w(gate + 2, grouped_w)
+            if gate >= 1:
+                activate(gate - 1, normed, tiles_at_once=BT)
+
         kept = keep.tile([P, BT * UNITS], F32)
-        nc.vector.tensor_tensor(out=kept[:], in0=gate_f[:], in1=c_raw[:], op=ALU.mult)
-        quantise_w(3)
-        gate_g = gate_output(2, ACT.Tanh, None)
+        nc.vector.tensor_tensor(out=kept[:], in0=gates[1][:], in1=c_raw[:], op=ALU.mult)
         fresh = keep.tile([P, BT * UNITS], F32)
-        nc.vector.tensor_tensor(out=fresh[:], in0=gate_i[:], in1=gate_g[:], op=ALU.mult)
+        nc.vector.tensor_tensor(out=fresh[:], in0=gates[0][:], in1=gates[2][:], op=ALU.mult)
         cell = keep.tile([P, BT * UNITS], F32)
         cell_sums = small.tile([P, BT], F32)
         for t in range(BT):
@@ -329,16 +371,23 @@ def tile_hyperlstmcell_pa_kernel(
                 op1=ALU.add,
                 accum_out=cell_sums[:, t : t + 1],
             )
-        gate_o = gate_output(3, ACT.Sigmoid, None)
+        cell_centred, cell_root = start_norm(cell, cell_sums, lnc_gamma)
+
+        normed = work.tile([P, BT * UNITS], F32, tag="normed")
+        finish_norm(started[3][0], started[3][1], ln_beta[:, gate_cols(3)], normed)
+        activate(3, normed, tiles_at_once=1)
+
         new_c = keep.tile([P, BT * UNITS], F32)
-        layer_norm(cell, cell_sums[:], lnc_gamma, lnc_beta, new_c)
-        nc.sync.dma_start(out=out_1.rearrange("(p t) n -> p (t n)", t=BT), in_=new_c[:])
+        finish_norm(cell_centred, cell_root, lnc_beta, new_c)
+        out_0_tiles = out_0.rearrange("(p t) n -> p t n", t=BT)
+        out_1_tiles = out_1.rearrange("(p t) n -> p t n", t=BT)
+        for t in range(BT):
+            nc.sync.dma_start(out=out_1_tiles[:, t, :], in_=new_c[:, block(t)])
         tanh_c = keep.tile([P, BT * UNITS], F32)
         new_h = keep.tile([P, BT * UNITS], F32)
-        out_0_tiles = out_0.rearrange("(p t) n -> p t n", t=BT)
         for t in range(BT):
             nc.scalar.activation(out=tanh_c[:, block(t)], in_=new_c[:, block(t)], func=ACT.Tanh)
             nc.vector.tensor_tensor(
-                out=new_h[:, block(t)], in0=tanh_c[:, block(t)], in1=gate_o[:, block(t)], op=ALU.mult
+                out=new_h[:, block(t)], in0=tanh_c[:, block(t)], in1=gates[3][:, block(t)], op=ALU.mult
             )
             nc.sync.dma_start(out=out_0_tiles[:, t, :], in_=new_h[:, block(t)])

@@ -223,17 +223,17 @@ def tile_hyperlstmcell_pa_kernel(
                 for g in range(0, PASSES, 2)
             ]
 
-        def quantise_w(gate, grouped_pair):
-            for i in range(2):
-                first = (gate * PASSES + 2 * i) * UNITS
-                cols = slice(first, first + 2 * UNITS)
-                nc.vector.quantize_mx(
-                    out=w_codes[:, cols].bitcast(FP8X4), scales=w_scales[:, cols], in_=grouped_pair[i][:]
-                )
+        def quantise_w(gate, i, grouped):
+            first = (gate * PASSES + 2 * i) * UNITS
+            cols = slice(first, first + 2 * UNITS)
+            nc.vector.quantize_mx(out=w_codes[:, cols].bitcast(FP8X4), scales=w_scales[:, cols], in_=grouped[:])
 
-        def start_norm(values, sums, gamma):
+        def negated_mean(sums):
             neg_mean = small.tile([P, BT], F32, tag="neg_mean")
             nc.vector.tensor_scalar_mul(out=neg_mean[:], in0=sums[:], scalar1=-1.0 / UNITS)
+            return neg_mean
+
+        def root_of_squares(values, neg_mean):
             sum_squares = small.tile([P, BT], F32, tag="sum_squares")
             squares = work.tile([P, BT * UNITS], F32, tag="squares")
             for t in range(BT):
@@ -244,6 +244,11 @@ def tile_hyperlstmcell_pa_kernel(
                     bias=neg_mean[:, t : t + 1],
                     accum_out=sum_squares[:, t : t + 1],
                 )
+            root = small.tile([P, BT], F32, tag="root")
+            nc.gpsimd.tensor_tensor(out=root[:], in0=sum_squares[:], in1=half_power[:], op=ALU.pow)
+            return root
+
+        def centre(values, neg_mean, gamma):
             centred = work.tile([P, BT * UNITS], F32, tag="centred")
             for t in range(BT):
                 nc.vector.scalar_tensor_tensor(
@@ -254,11 +259,9 @@ def tile_hyperlstmcell_pa_kernel(
                     op0=ALU.add,
                     op1=ALU.mult,
                 )
-            root = small.tile([P, BT], F32, tag="root")
-            nc.gpsimd.tensor_tensor(out=root[:], in0=sum_squares[:], in1=half_power[:], op=ALU.pow)
-            return centred, root
+            return centred
 
-        def finish_norm(centred, root, beta, out):
+        def std_plus_eps(root):
             std_eps = small.tile([P, BT], F32, tag="std_eps")
             nc.vector.tensor_scalar(
                 out=std_eps[:],
@@ -268,8 +271,14 @@ def tile_hyperlstmcell_pa_kernel(
                 op0=ALU.mult,
                 op1=ALU.add,
             )
+            return std_eps
+
+        def inverse(std_eps):
             inv_std = small.tile([P, BT], F32, tag="inv_std")
             nc.vector.reciprocal(out=inv_std[:], in_=std_eps[:])
+            return inv_std
+
+        def scale_and_shift(centred, inv_std, beta, out):
             for t in range(BT):
                 nc.vector.scalar_tensor_tensor(
                     out=out[:, block(t)],
@@ -336,24 +345,35 @@ def tile_hyperlstmcell_pa_kernel(
         grouped_u = grouped_u + [flip_u(2), flip_u(3)]
         quantise_u(2, grouped_u[2])
         quantise_u(3, grouped_u[3])
-        quantise_w(0, flip_w(0, vector_helps=True))
-        quantise_w(1, flip_w(1, vector_helps=False))
+        grouped_w = {0: flip_w(0, vector_helps=True)}
+        quantise_w(0, 0, grouped_w[0][0])
+        quantise_w(0, 1, grouped_w[0][1])
+        grouped_w[1] = flip_w(1, vector_helps=False)
 
-        started = []
+        roots = []
+        centreds = []
         for gate in range(GATES):
+            before = gate - 1
             v, v_sums = gate_sums(gate)
-            started.append(start_norm(v, v_sums, ln_gamma[:, gate_cols(gate)]))
-            if gate >= 1:
-                normed = work.tile([P, BT * UNITS], F32, tag="normed")
-                finish_norm(started[gate - 1][0], started[gate - 1][1], ln_beta[:, gate_cols(gate - 1)], normed)
-            if gate + 2 < GATES:
-                grouped_w = flip_w(gate + 2, vector_helps=False)
             if gate + 1 < GATES:
                 plain_product(gate + 1)
+                quantise_w(gate + 1, 0, grouped_w[gate + 1][0])
+            neg_mean = negated_mean(v_sums)
+            if before >= 0:
+                std_eps = std_plus_eps(roots[before])
+            roots.append(root_of_squares(v, neg_mean))
+            if gate + 1 < GATES:
+                quantise_w(gate + 1, 1, grouped_w[gate + 1][1])
+            if before >= 0:
+                inv_std = inverse(std_eps)
+            centreds.append(centre(v, neg_mean, ln_gamma[:, gate_cols(gate)]))
+            if before >= 0:
+                normed = work.tile([P, BT * UNITS], F32, tag="normed")
+                scale_and_shift(centreds[before], inv_std, ln_beta[:, gate_cols(before)], normed)
             if gate + 2 < GATES:
-                quantise_w(gate + 2, grouped_w)
-            if gate >= 1:
-                activate(gate - 1, normed, tiles_at_once=BT)
+                grouped_w[gate + 2] = flip_w(gate + 2, vector_helps=False)
+            if before >= 0:
+                activate(before, normed, tiles_at_once=BT)
 
         kept = keep.tile([P, BT * UNITS], F32)
         nc.vector.tensor_tensor(out=kept[:], in0=gates[1][:], in1=c_raw[:], op=ALU.mult)
@@ -371,14 +391,17 @@ def tile_hyperlstmcell_pa_kernel(
                 op1=ALU.add,
                 accum_out=cell_sums[:, t : t + 1],
             )
-        cell_centred, cell_root = start_norm(cell, cell_sums, lnc_gamma)
-
+        std_eps = std_plus_eps(roots[3])
+        cell_neg_mean = negated_mean(cell_sums)
+        inv_std = inverse(std_eps)
+        cell_root = root_of_squares(cell, cell_neg_mean)
+        cell_centred = centre(cell, cell_neg_mean, lnc_gamma)
         normed = work.tile([P, BT * UNITS], F32, tag="normed")
-        finish_norm(started[3][0], started[3][1], ln_beta[:, gate_cols(3)], normed)
+        scale_and_shift(centreds[3], inv_std, ln_beta[:, gate_cols(3)], normed)
         activate(3, normed, tiles_at_once=1)
 
         new_c = keep.tile([P, BT * UNITS], F32)
-        finish_norm(cell_centred, cell_root, lnc_beta, new_c)
+        scale_and_shift(cell_centred, inverse(std_plus_eps(cell_root)), lnc_beta, new_c)
         out_0_tiles = out_0.rearrange("(p t) n -> p t n", t=BT)
         out_1_tiles = out_1.rearrange("(p t) n -> p t n", t=BT)
         for t in range(BT):

@@ -80,14 +80,13 @@ def tile_hyperlstmcell_pa_kernel(
         table_warmer = consts.tile([P, 1], F32)
         nc.scalar.activation(out=table_warmer[:], in_=one_column[:], func=ACT.Sigmoid)
 
+        hh_raw = raw.tile([P, BT * UNITS], BF16)
+        nc.sync.dma_start(out=hh_raw[:], in_=hyper_h.rearrange("(p t) k -> p (t k)", t=BT))
         nc.sync.dma_start(out=norm_rows[0:8, :], in_=hc_ln_gamma.rearrange("g (c q) -> (g c) q", q=P))
         nc.sync.dma_start(out=norm_rows[8:16, :], in_=hc_ln_beta.rearrange("g (c q) -> (g c) q", q=P))
         nc.sync.dma_start(out=norm_rows[16:18, :], in_=hc_lnc_gamma.rearrange("(c q) -> c q", q=P))
         nc.sync.dma_start(out=norm_rows[18:20, :], in_=hc_lnc_beta.rearrange("(c q) -> c q", q=P))
-        NORM_CHUNKS = 20
         nc.sync.dma_start(out=bias_row[0:1, :], in_=hc_bih.rearrange("(o n) -> o n", o=1))
-        hh_raw = raw.tile([P, BT * UNITS], BF16)
-        nc.sync.dma_start(out=hh_raw[:], in_=hyper_h.rearrange("(p t) k -> p (t k)", t=BT))
         whh_raw = raw.tile([P, (N // P) * UNITS], BF16)
         nc.sync.dma_start(
             out=whh_raw[:].rearrange("p (j k) -> p j k", k=UNITS),
@@ -109,29 +108,6 @@ def tile_hyperlstmcell_pa_kernel(
             if gate == 1:
                 nc.sync.dma_start(out=c_raw[:], in_=hyper_c.rearrange("(p t) n -> p (t n)", t=BT))
 
-        norm_cols_psum = flip_psum.tile([P, 2 * BANK], BF16, tag="flip")
-        nc.tensor.transpose(out=norm_cols_psum[:, 0:P], in_=norm_rows[:], identity=ident_bf16[:])
-        norm_cols = consts.tile([P, P], BF16)
-        nc.vector.tensor_copy(out=norm_cols[:], in_=norm_cols_psum[:, 0:P])
-        norm_all = consts.tile([P, NORM_CHUNKS * P], BF16)
-        CHUNKS_PER_BANK = 2 * BANK // P
-        for first in range(0, NORM_CHUNKS, CHUNKS_PER_BANK):
-            chunks = min(CHUNKS_PER_BANK, NORM_CHUNKS - first)
-            spread = flip_psum.tile([P, 2 * BANK], BF16, tag="flip")
-            for i in range(chunks):
-                nc.tensor.transpose(
-                    out=spread[:, i * P : (i + 1) * P],
-                    in_=norm_cols[:, first + i : first + i + 1].to_broadcast([P, P]),
-                    identity=ident_bf16[:],
-                )
-            nc.vector.tensor_copy(
-                out=norm_all[:, first * P : (first + chunks) * P], in_=spread[:, 0 : chunks * P]
-            )
-        ln_gamma = norm_all[:, 0:N]
-        ln_beta = norm_all[:, N : 2 * N]
-        lnc_gamma = norm_all[:, 2 * N : 2 * N + UNITS]
-        lnc_beta = norm_all[:, 2 * N + UNITS : 2 * N + 2 * UNITS]
-
         hh_t = operands.tile([P, KH * BT * P], BF16)
         hh_t_psum = flip_psum.tile([P, 2 * BANK], BF16, tag="flip")
         for step in range(KH):
@@ -142,6 +118,36 @@ def tile_hyperlstmcell_pa_kernel(
                     identity=ident_bf16[:],
                 )
         nc.vector.tensor_copy(out=hh_t[:], in_=hh_t_psum[:])
+
+        norm_cols_psum = flip_psum.tile([P, 2 * BANK], BF16, tag="flip")
+        nc.tensor.transpose(out=norm_cols_psum[:, 0:P], in_=norm_rows[:], identity=ident_bf16[:])
+        norm_cols = consts.tile([P, P], BF16)
+        nc.vector.tensor_copy(out=norm_cols[:], in_=norm_cols_psum[:, 0:P])
+        norm_cols_f32 = consts.tile([P, P], F32)
+        nc.vector.tensor_copy(out=norm_cols_f32[:], in_=norm_cols_psum[:, 0:P])
+        GAMMA_CHUNK = 0
+        BETA_CHUNK = N // P
+        LNC_GAMMA_CHUNK = 2 * N // P
+        LNC_BETA_CHUNK = 2 * N // P + UNITS // P
+        GATE_CHUNKS = UNITS // P
+
+        def spread_chunks(bank, first, chunks):
+            for i in range(chunks):
+                nc.tensor.transpose(
+                    out=bank[:, i * P : (i + 1) * P],
+                    in_=norm_cols[:, first + i : first + i + 1].to_broadcast([P, P]),
+                    identity=ident_bf16[:],
+                )
+
+        VECTOR_GATES = 2
+        spread = flip_psum.tile([P, 2 * BANK], BF16, tag="flip")
+        spread_chunks(spread[:, 0 : VECTOR_GATES * UNITS], GAMMA_CHUNK, VECTOR_GATES * GATE_CHUNKS)
+        spread_chunks(spread[:, VECTOR_GATES * UNITS :], BETA_CHUNK, VECTOR_GATES * GATE_CHUNKS)
+        ln_vectors = consts.tile([P, 2 * VECTOR_GATES * UNITS], BF16)
+        nc.vector.tensor_copy(out=ln_vectors[:], in_=spread[:])
+        ln_gamma = ln_vectors[:, 0 : VECTOR_GATES * UNITS]
+        ln_beta = ln_vectors[:, VECTOR_GATES * UNITS :]
+
         whh_t = operands.tile([P, KH * N], BF16)
         for step in range(KH):
             whh_t_psum = flip_psum.tile([P, 2 * BANK], BF16, tag="flip")
@@ -233,20 +239,26 @@ def tile_hyperlstmcell_pa_kernel(
             nc.vector.tensor_scalar_mul(out=neg_mean[:], in0=sums[:], scalar1=-1.0 / UNITS)
             return neg_mean
 
+        def sum_of_squares(values, neg_mean, squares, sum_squares, t):
+            nc.scalar.activation(
+                out=squares[:, block(t)],
+                in_=values[:, block(t)],
+                func=ACT.Square,
+                bias=neg_mean[:, t : t + 1],
+                accum_out=sum_squares[:, t : t + 1],
+            )
+
+        def square_root(sum_squares):
+            root = small.tile([P, BT], F32, tag="root")
+            nc.gpsimd.tensor_tensor(out=root[:], in0=sum_squares[:], in1=half_power[:], op=ALU.pow)
+            return root
+
         def root_of_squares(values, neg_mean):
             sum_squares = small.tile([P, BT], F32, tag="sum_squares")
             squares = work.tile([P, BT * UNITS], F32, tag="squares")
             for t in range(BT):
-                nc.scalar.activation(
-                    out=squares[:, block(t)],
-                    in_=values[:, block(t)],
-                    func=ACT.Square,
-                    bias=neg_mean[:, t : t + 1],
-                    accum_out=sum_squares[:, t : t + 1],
-                )
-            root = small.tile([P, BT], F32, tag="root")
-            nc.gpsimd.tensor_tensor(out=root[:], in0=sum_squares[:], in1=half_power[:], op=ALU.pow)
-            return root
+                sum_of_squares(values, neg_mean, squares, sum_squares, t)
+            return square_root(sum_squares)
 
         def centre(values, neg_mean, gamma):
             centred = work.tile([P, BT * UNITS], F32, tag="centred")
@@ -324,19 +336,67 @@ def tile_hyperlstmcell_pa_kernel(
         def gate_cols(gate):
             return slice(gate * UNITS, (gate + 1) * UNITS)
 
-        GATE_FUNC = [ACT.Sigmoid, ACT.Sigmoid, ACT.Tanh, ACT.Sigmoid]
-        gates = [keep.tile([P, BT * UNITS], F32, name="gate%d" % gate) for gate in range(GATES)]
+        gates = [keep.tile([P, BT * UNITS], F32, name="gate%d" % gate) for gate in range(VECTOR_GATES)]
 
-        def activate(gate, normed, tiles_at_once):
-            width = tiles_at_once * UNITS
-            for first in range(0, BT * UNITS, width):
-                cols = slice(first, first + width)
-                if gate == 1:
+        def activate(gate, normed):
+            if gate == 1:
+                nc.scalar.activation(out=gates[gate][:], in_=normed[:], func=ACT.Sigmoid, bias=one_column[:])
+            else:
+                nc.scalar.activation(out=gates[gate][:], in_=normed[:], func=ACT.Sigmoid)
+
+        def row_scale_and_bias(neg_mean, root):
+            inv_std = inverse(std_plus_eps(root))
+            neg_mean_over_std = small.tile([P, BT], F32, tag="neg_mean_over_std")
+            nc.vector.tensor_tensor(out=neg_mean_over_std[:], in0=neg_mean[:], in1=inv_std[:], op=ALU.mult)
+            return inv_std, neg_mean_over_std
+
+        def gate_by_transposes(gate, func, v, inv_std, neg_mean_over_std, result_psum, result_tag):
+            normed = work.tile([P, BT * UNITS], F32, tag="normed")
+            flipped = []
+            for pair in range(BT // 2):
+                bank = flip_psum.tile([P, BANK], F32, tag="flip")
+                for i in range(2):
+                    t = 2 * pair + i
                     nc.scalar.activation(
-                        out=gates[gate][:, cols], in_=normed[:, cols], func=GATE_FUNC[gate], bias=one_column[:]
+                        out=normed[:, block(t)],
+                        in_=v[:, block(t)],
+                        func=ACT.Identity,
+                        scale=inv_std[:, t : t + 1],
+                        bias=neg_mean_over_std[:, t : t + 1],
                     )
-                else:
-                    nc.scalar.activation(out=gates[gate][:, cols], in_=normed[:, cols], func=GATE_FUNC[gate])
+                for c in range(GATE_CHUNKS):
+                    for i in range(2):
+                        t = 2 * pair + i
+                        nc.tensor.transpose(
+                            out=bank[:, (2 * c + i) * P : (2 * c + i + 1) * P],
+                            in_=normed[:, t * UNITS + c * P : t * UNITS + (c + 1) * P],
+                            identity=ident_f32[:],
+                        )
+                flipped.append(bank)
+            gate_t = work.tile([P, BT * UNITS], F32, tag="gate_t")
+            result = []
+            for pair in range(BT // 2):
+                for c in range(GATE_CHUNKS):
+                    gamma_chunk = GAMMA_CHUNK + gate * GATE_CHUNKS + c
+                    beta_chunk = BETA_CHUNK + gate * GATE_CHUNKS + c
+                    nc.scalar.activation(
+                        out=gate_t[:, (2 * pair + c) * UNITS : (2 * pair + c + 1) * UNITS],
+                        in_=flipped[pair][:, c * UNITS : (c + 1) * UNITS],
+                        func=func,
+                        scale=norm_cols_f32[:, gamma_chunk : gamma_chunk + 1],
+                        bias=norm_cols_f32[:, beta_chunk : beta_chunk + 1],
+                    )
+                bank = result_psum.tile([P, BANK], F32, tag=result_tag)
+                for i in range(2):
+                    for c in range(GATE_CHUNKS):
+                        first = (2 * pair + c) * UNITS + i * P
+                        nc.tensor.transpose(
+                            out=bank[:, i * UNITS + c * P : i * UNITS + (c + 1) * P],
+                            in_=gate_t[:, first : first + P],
+                            identity=ident_f32[:],
+                        )
+                result.append(bank)
+            return result
 
         grouped_u = [flip_u(0), flip_u(1)]
         quantise_u(0, grouped_u[0])
@@ -350,56 +410,77 @@ def tile_hyperlstmcell_pa_kernel(
         quantise_w(0, 1, grouped_w[0][1])
         grouped_w[1] = flip_w(1, vector_helps=False)
 
+        vs = []
+        neg_means = []
         roots = []
         centreds = []
-        for gate in range(GATES):
+        for gate in range(GATES - 1):
             before = gate - 1
             v, v_sums = gate_sums(gate)
-            if gate + 1 < GATES:
-                plain_product(gate + 1)
-                quantise_w(gate + 1, 0, grouped_w[gate + 1][0])
-            neg_mean = negated_mean(v_sums)
+            vs.append(v)
+            neg_means.append(negated_mean(v_sums))
+            roots.append(root_of_squares(v, neg_means[gate]))
+            plain_product(gate + 1)
+            quantise_w(gate + 1, 0, grouped_w[gate + 1][0])
             if before >= 0:
                 std_eps = std_plus_eps(roots[before])
-            roots.append(root_of_squares(v, neg_mean))
-            if gate + 1 < GATES:
-                quantise_w(gate + 1, 1, grouped_w[gate + 1][1])
+            quantise_w(gate + 1, 1, grouped_w[gate + 1][1])
             if before >= 0:
                 inv_std = inverse(std_eps)
-            centreds.append(centre(v, neg_mean, ln_gamma[:, gate_cols(gate)]))
+            if gate < VECTOR_GATES:
+                centreds.append(centre(v, neg_means[gate], ln_gamma[:, gate_cols(gate)]))
             if before >= 0:
                 normed = work.tile([P, BT * UNITS], F32, tag="normed")
                 scale_and_shift(centreds[before], inv_std, ln_beta[:, gate_cols(before)], normed)
             if gate + 2 < GATES:
                 grouped_w[gate + 2] = flip_w(gate + 2, vector_helps=False)
             if before >= 0:
-                activate(before, normed, tiles_at_once=BT)
+                activate(before, normed)
 
+        late = flip_psum.tile([P, 2 * BANK], BF16, tag="flip")
+        spread_chunks(late[:, 0:UNITS], LNC_GAMMA_CHUNK, GATE_CHUNKS)
+        spread_chunks(late[:, UNITS : 2 * UNITS], LNC_BETA_CHUNK, GATE_CHUNKS)
+        lnc_gamma = late[:, 0:UNITS]
+        lnc_beta = late[:, UNITS : 2 * UNITS]
+
+        inv_std, neg_mean_over_std = row_scale_and_bias(neg_means[2], roots[2])
+        v, v_sums = gate_sums(3)
+        gate_g = gate_by_transposes(2, ACT.Tanh, vs[2], inv_std, neg_mean_over_std, mx_psum, "mx")
+        neg_mean = negated_mean(v_sums)
         kept = keep.tile([P, BT * UNITS], F32)
         nc.vector.tensor_tensor(out=kept[:], in0=gates[1][:], in1=c_raw[:], op=ALU.mult)
+        root = root_of_squares(v, neg_mean)
+
         fresh = keep.tile([P, BT * UNITS], F32)
-        nc.vector.tensor_tensor(out=fresh[:], in0=gates[0][:], in1=gates[2][:], op=ALU.mult)
+        for pair in range(BT // 2):
+            cols = slice(pair * BANK, (pair + 1) * BANK)
+            nc.vector.tensor_tensor(out=fresh[:, cols], in0=gates[0][:, cols], in1=gate_g[pair][:], op=ALU.mult)
         cell = keep.tile([P, BT * UNITS], F32)
         cell_sums = small.tile([P, BT], F32)
-        for t in range(BT):
-            nc.vector.scalar_tensor_tensor(
-                out=cell[:, block(t)],
-                in0=kept[:, block(t)],
-                scalar=1.0,
-                in1=fresh[:, block(t)],
-                op0=ALU.mult,
-                op1=ALU.add,
-                accum_out=cell_sums[:, t : t + 1],
-            )
-        std_eps = std_plus_eps(roots[3])
-        cell_neg_mean = negated_mean(cell_sums)
-        inv_std = inverse(std_eps)
-        cell_root = root_of_squares(cell, cell_neg_mean)
-        cell_centred = centre(cell, cell_neg_mean, lnc_gamma)
-        normed = work.tile([P, BT * UNITS], F32, tag="normed")
-        scale_and_shift(centreds[3], inv_std, ln_beta[:, gate_cols(3)], normed)
-        activate(3, normed, tiles_at_once=1)
+        cell_neg_mean = small.tile([P, BT], F32)
+        cell_sum_squares = small.tile([P, BT], F32)
+        squares = work.tile([P, BT * UNITS], F32, tag="squares")
+        for t in range(BT + 1):
+            if t < BT:
+                nc.vector.scalar_tensor_tensor(
+                    out=cell[:, block(t)],
+                    in0=kept[:, block(t)],
+                    scalar=1.0,
+                    in1=fresh[:, block(t)],
+                    op0=ALU.mult,
+                    op1=ALU.add,
+                    accum_out=cell_sums[:, t : t + 1],
+                )
+            if t >= 1:
+                done = slice(t - 1, t)
+                nc.vector.tensor_scalar_mul(out=cell_neg_mean[:, done], in0=cell_sums[:, done], scalar1=-1.0 / UNITS)
+                sum_of_squares(cell, cell_neg_mean, squares, cell_sum_squares, t - 1)
+        cell_root = square_root(cell_sum_squares)
 
+        inv_std, neg_mean_over_std = row_scale_and_bias(neg_mean, root)
+        gate_o = gate_by_transposes(3, ACT.Sigmoid, v, inv_std, neg_mean_over_std, plain_psum, "plain")
+
+        cell_centred = centre(cell, cell_neg_mean, lnc_gamma)
         new_c = keep.tile([P, BT * UNITS], F32)
         scale_and_shift(cell_centred, inverse(std_plus_eps(cell_root)), lnc_beta, new_c)
         out_0_tiles = out_0.rearrange("(p t) n -> p t n", t=BT)
@@ -411,6 +492,9 @@ def tile_hyperlstmcell_pa_kernel(
         for t in range(BT):
             nc.scalar.activation(out=tanh_c[:, block(t)], in_=new_c[:, block(t)], func=ACT.Tanh)
             nc.vector.tensor_tensor(
-                out=new_h[:, block(t)], in0=tanh_c[:, block(t)], in1=gates[3][:, block(t)], op=ALU.mult
+                out=new_h[:, block(t)],
+                in0=tanh_c[:, block(t)],
+                in1=gate_o[t // 2][:, (t % 2) * UNITS : (t % 2 + 1) * UNITS],
+                op=ALU.mult,
             )
             nc.sync.dma_start(out=out_0_tiles[:, t, :], in_=new_h[:, block(t)])

import math
from contextlib import ExitStack

import concourse.mybir as mybir
from concourse.masks import make_identity

F32 = mybir.dt.float32
BF16 = mybir.dt.bfloat16
U32 = mybir.dt.uint32
U8 = mybir.dt.uint8
FP8X4 = mybir.dt.float8_e4m3fn_x4
ALU = mybir.AluOpType
ACT = mybir.ActivationFunctionType

P = 128
BATCH = 512
BT = BATCH // P
IN = 1024
K = 2 * IN
UNITS = 256
GATES = 4
N = GATES * UNITS
KH = UNITS // P
K_PASS = 4 * P
PASSES = K // K_PASS
PASS_WORDS = K_PASS // 2
BANK = 512
EPS = 1e-6

FLOPS = 2 * BATCH * N * K + 2 * BATCH * N * UNITS


def tile_hyperlstmcell_pa_kernel(
    tc,
    x,
    h,
    hyper_h,
    hyper_c,
    hc_Wih,
    hc_bih,
    hc_Whh,
    hc_ln_gamma,
    hc_ln_beta,
    hc_lnc_gamma,
    hc_lnc_beta,
    out_0,
    out_1,
):
    nc = tc.nc
    with ExitStack() as stack:
        stack.enter_context(tc.manual_schedule())
        consts = stack.enter_context(tc.tile_pool(name="consts", bufs=1))
        raw = stack.enter_context(tc.tile_pool(name="raw", bufs=1))
        operands = stack.enter_context(tc.tile_pool(name="operands", bufs=1))
        stage = stack.enter_context(tc.tile_pool(name="stage", bufs=4))
        work = stack.enter_context(tc.tile_pool(name="work", bufs=2))
        small = stack.enter_context(tc.tile_pool(name="small", bufs=3))
        keep = stack.enter_context(tc.tile_pool(name="keep", bufs=1))
        flip_psum = stack.enter_context(tc.psum_pool(name="flip_psum", bufs=4))
        mx_psum = stack.enter_context(tc.psum_pool(name="mx_psum", bufs=2))
        plain_psum = stack.enter_context(tc.psum_pool(name="plain_psum", bufs=2))

        def block(t):
            return slice(t * UNITS, (t + 1) * UNITS)

        norm_rows = consts.tile([P, P], BF16)
        nc.vector.memset(norm_rows[:], 0.0)
        bias_row = consts.tile([P, N], BF16)
        nc.vector.memset(bias_row[:], 0.0)
        ones = consts.tile([P, P], BF16)
        nc.vector.memset(ones[:], 1.0)
        half_power = consts.tile([P, BT], F32)
        nc.vector.memset(half_power[:], 0.5)
        one_column = consts.tile([P, 1], F32)
        nc.vector.memset(one_column[:], 1.0)
        ident_bf16 = consts.tile([P, P], BF16)
        make_identity(nc, ident_bf16[:])
        ident_f32 = consts.tile([P, P], F32)
        make_identity(nc, ident_f32[:])
        table_warmer = consts.tile([P, 1], F32)
        nc.scalar.activation(out=table_warmer[:], in_=one_column[:], func=ACT.Sigmoid)

        hh_raw = raw.tile([P, BT * UNITS], BF16)
        nc.sync.dma_start(out=hh_raw[:], in_=hyper_h.rearrange("(p t) k -> p (t k)", t=BT))
        nc.sync.dma_start(out=norm_rows[0:8, :], in_=hc_ln_gamma.rearrange("g (c q) -> (g c) q", q=P))
        nc.sync.dma_start(out=norm_rows[8:16, :], in_=hc_ln_beta.rearrange("g (c q) -> (g c) q", q=P))
        nc.sync.dma_start(out=norm_rows[16:18, :], in_=hc_lnc_gamma.rearrange("(c q) -> c q", q=P))
        nc.sync.dma_start(out=norm_rows[18:20, :], in_=hc_lnc_beta.rearrange("(c q) -> c q", q=P))
        nc.sync.dma_start(out=bias_row[0:1, :], in_=hc_bih.rearrange("(o n) -> o n", o=1))
        whh_raw = raw.tile([P, (N // P) * UNITS], BF16)
        nc.sync.dma_start(
            out=whh_raw[:].rearrange("p (j k) -> p j k", k=UNITS),
            in_=hc_Whh.rearrange("(j p) k -> p j k", p=P),
        )
        x_raw = raw.tile([P, BT * IN], BF16)
        nc.sync.dma_start(out=x_raw[:], in_=x.rearrange("(p t) k -> p (t k)", t=BT))
        h_raw = raw.tile([P, BT * IN], BF16)
        nc.sync.dma_start(out=h_raw[:], in_=h.rearrange("(p t) k -> p (t k)", t=BT))
        c_raw = raw.tile([P, BT * UNITS], BF16)
        w_raw = []
        for gate in range(GATES):
            w_gate = raw.tile([P, 2 * K], BF16, name="w_raw%d" % gate)
            nc.sync.dma_start(
                out=w_gate[:].rearrange("p (j k) -> p j k", k=K),
                in_=hc_Wih[gate * UNITS : (gate + 1) * UNITS, :].rearrange("(j p) k -> p j k", p=P),
            )
            w_raw.append(w_gate)
            if gate == 1:
                nc.sync.dma_start(out=c_raw[:], in_=hyper_c.rearrange("(p t) n -> p (t n)", t=BT))

        hh_t = operands.tile([P, KH * BT * P], BF16)
        hh_t_psum = flip_psum.tile([P, 2 * BANK], BF16, tag="flip")
        for step in range(KH):
            for t in range(BT):
                nc.tensor.transpose(
                    out=hh_t_psum[:, (step * BT + t) * P : (step * BT + t + 1) * P],
                    in_=hh_raw[:, t * UNITS + step * P : t * UNITS + (step + 1) * P],
                    identity=ident_bf16[:],
                )
        nc.vector.tensor_copy(out=hh_t[:], in_=hh_t_psum[:])

        norm_cols_psum = flip_psum.tile([P, 2 * BANK], BF16, tag="flip")
        nc.tensor.transpose(out=norm_cols_psum[:, 0:P], in_=norm_rows[:], identity=ident_bf16[:])
        norm_cols = consts.tile([P, P], BF16)
        nc.vector.tensor_copy(out=norm_cols[:], in_=norm_cols_psum[:, 0:P])
        norm_cols_f32 = consts.tile([P, P], F32)
        nc.vector.tensor_copy(out=norm_cols_f32[:], in_=norm_cols_psum[:, 0:P])
        GAMMA_CHUNK = 0
        BETA_CHUNK = N // P
        LNC_GAMMA_CHUNK = 2 * N // P
        LNC_BETA_CHUNK = 2 * N // P + UNITS // P
        GATE_CHUNKS = UNITS // P

        def spread_chunks(bank, first, chunks):
            for i in range(chunks):
                nc.tensor.transpose(
                    out=bank[:, i * P : (i + 1) * P],
                    in_=norm_cols[:, first + i : first + i + 1].to_broadcast([P, P]),
                    identity=ident_bf16[:],
                )

        VECTOR_GATES = 2
        spread = flip_psum.tile([P, 2 * BANK], BF16, tag="flip")
        spread_chunks(spread[:, 0 : VECTOR_GATES * UNITS], GAMMA_CHUNK, VECTOR_GATES * GATE_CHUNKS)
        spread_chunks(spread[:, VECTOR_GATES * UNITS :], BETA_CHUNK, VECTOR_GATES * GATE_CHUNKS)
        ln_vectors = consts.tile([P, 2 * VECTOR_GATES * UNITS], BF16)
        nc.vector.tensor_copy(out=ln_vectors[:], in_=spread[:])
        ln_gamma = ln_vectors[:, 0 : VECTOR_GATES * UNITS]
        ln_beta = ln_vectors[:, VECTOR_GATES * UNITS :]

        whh_t = operands.tile([P, KH * N], BF16)
        for step in range(KH):
            whh_t_psum = flip_psum.tile([P, 2 * BANK], BF16, tag="flip")
            for j in range(N // P):
                nc.tensor.transpose(
                    out=whh_t_psum[:, j * P : (j + 1) * P],
                    in_=whh_raw[:, j * UNITS + step * P : j * UNITS + (step + 1) * P],
                    identity=ident_bf16[:],
                )
            if step == 0:
                nc.vector.tensor_copy(out=whh_t[:, step * N : (step + 1) * N], in_=whh_t_psum[:])
            else:
                nc.scalar.copy(out=whh_t[:, step * N : (step + 1) * N], in_=whh_t_psum[:])

        plain = operands.tile([P, GATES * BT * UNITS], F32)

        def plain_product(gate):
            units = slice(gate * UNITS, (gate + 1) * UNITS)
            for pair in range(BT // 2):
                bank = plain_psum.tile([P, BANK], F32, tag="plain")
                for i in range(2):
                    t = 2 * pair + i
                    group = bank[:, i * UNITS : (i + 1) * UNITS]
                    for step in range(KH):
                        nc.tensor.matmul(
                            out=group,
                            lhsT=hh_t[:, (step * BT + t) * P : (step * BT + t + 1) * P],
                            rhs=whh_t[:, step * N + gate * UNITS : step * N + (gate + 1) * UNITS],
                            start=(step == 0),
                            stop=False,
                        )
                    nc.tensor.matmul(out=group, lhsT=ones[:], rhs=bias_row[:, units], start=False, stop=True)
                first = (gate * BT + 2 * pair) * UNITS
                nc.scalar.copy(out=plain[:, first : first + BANK], in_=bank[:])

        u_codes = operands.tile([P, PASSES * BATCH], U32, align_bytes=64)
        u_scales = operands.tile([P, PASSES * BATCH], U8, align_bytes=64)
        w_codes = operands.tile([P, GATES * PASSES * UNITS], U32, align_bytes=64)
        w_scales = operands.tile([P, GATES * PASSES * UNITS], U8, align_bytes=64)

        def flip(pieces, vector_helps):
            grouped = stage.tile([P, 2 * BANK * 2], BF16, align_bytes=64, tag="grouped")
            grouped_words = grouped[:].bitcast(F32)
            for b in range(2):
                row_tiles, first_word = pieces[b]
                bank = flip_psum.tile([P, BANK], F32, tag="flip")
                for half in range(2):
                    for i in range(2):
                        nc.tensor.transpose(
                            out=bank[:, (2 * half + i) * P : (2 * half + i + 1) * P],
                            in_=row_tiles[i][:, first_word + half * P : first_word + (half + 1) * P],
                            identity=ident_f32[:],
                        )
                side_by_side = grouped_words[:, b * BANK : (b + 1) * BANK].rearrange("p (r u) -> p r u", u=2)
                halves = bank[:].rearrange("p (u r) -> p r u", u=2)
                if vector_helps and b == 0:
                    nc.vector.tensor_copy(out=side_by_side, in_=halves)
                else:
                    nc.scalar.copy(out=side_by_side, in_=halves)
            return grouped

        def flip_u(g):
            source = (x_raw if g < PASSES // 2 else h_raw)[:].bitcast(F32)
            row_words = IN // 2
            first_word = (g % (PASSES // 2)) * PASS_WORDS
            tiles = [source[:, t * row_words : (t + 1) * row_words] for t in range(BT)]
            return flip([(tiles[0:2], first_word), (tiles[2:4], first_word)], vector_helps=True)

        def quantise_u(g, grouped):
            cols = slice(g * BATCH, (g + 1) * BATCH)
            nc.vector.quantize_mx(out=u_codes[:, cols].bitcast(FP8X4), scales=u_scales[:, cols], in_=grouped[:])

        def flip_w(gate, vector_helps):
            source = w_raw[gate][:].bitcast(F32)
            row_words = K // 2
            tiles = [source[:, j * row_words : (j + 1) * row_words] for j in range(2)]
            return [
                flip([(tiles, g * PASS_WORDS), (tiles, (g + 1) * PASS_WORDS)], vector_helps)
                for g in range(0, PASSES, 2)
            ]

        def quantise_w(gate, i, grouped):
            first = (gate * PASSES + 2 * i) * UNITS
            cols = slice(first, first + 2 * UNITS)
            nc.vector.quantize_mx(out=w_codes[:, cols].bitcast(FP8X4), scales=w_scales[:, cols], in_=grouped[:])

        def negated_mean(sums):
            neg_mean = small.tile([P, BT], F32, tag="neg_mean")
            nc.vector.tensor_scalar_mul(out=neg_mean[:], in0=sums[:], scalar1=-1.0 / UNITS)
            return neg_mean

        def sum_of_squares(values, neg_mean, squares, sum_squares, t):
            nc.scalar.activation(
                out=squares[:, block(t)],
                in_=values[:, block(t)],
                func=ACT.Square,
                bias=neg_mean[:, t : t + 1],
                accum_out=sum_squares[:, t : t + 1],
            )

        def square_root(sum_squares):
            root = small.tile([P, BT], F32, tag="root")
            nc.gpsimd.tensor_tensor(out=root[:], in0=sum_squares[:], in1=half_power[:], op=ALU.pow)
            return root

        def root_of_squares(values, neg_mean):
            sum_squares = small.tile([P, BT], F32, tag="sum_squares")
            squares = work.tile([P, BT * UNITS], F32, tag="squares")
            for t in range(BT):
                sum_of_squares(values, neg_mean, squares, sum_squares, t)
            return square_root(sum_squares)

        def centre(values, neg_mean, gamma):
            centred = work.tile([P, BT * UNITS], F32, tag="centred")
            for t in range(BT):
                nc.vector.scalar_tensor_tensor(
                    out=centred[:, block(t)],
                    in0=values[:, block(t)],
                    scalar=neg_mean[:, t : t + 1],
                    in1=gamma,
                    op0=ALU.add,
                    op1=ALU.mult,
                )
            return centred

        def std_plus_eps(root):
            std_eps = small.tile([P, BT], F32, tag="std_eps")
            nc.vector.tensor_scalar(
                out=std_eps[:],
                in0=root[:],
                scalar1=1.0 / math.sqrt(UNITS - 1),
                scalar2=EPS,
                op0=ALU.mult,
                op1=ALU.add,
            )
            return std_eps

        def inverse(std_eps):
            inv_std = small.tile([P, BT], F32, tag="inv_std")
            nc.vector.reciprocal(out=inv_std[:], in_=std_eps[:])
            return inv_std

        def scale_and_shift(centred, inv_std, beta, out):
            for t in range(BT):
                nc.vector.scalar_tensor_tensor(
                    out=out[:, block(t)],
                    in0=centred[:, block(t)],
                    scalar=inv_std[:, t : t + 1],
                    in1=beta,
                    op0=ALU.mult,
                    op1=ALU.add,
                )

        def gate_sums(gate):
            v = work.tile([P, BT * UNITS], F32, tag="v")
            v_sums = small.tile([P, BT], F32, tag="v_sums")
            for pair in range(BT // 2):
                bank = mx_psum.tile([P, BANK], F32, tag="mx")
                for i in range(2):
                    t = 2 * pair + i
                    for g in range(PASSES):
                        u_cols = slice(g * BATCH + t * P, g * BATCH + (t + 1) * P)
                        w_cols = slice((gate * PASSES + g) * UNITS, (gate * PASSES + g + 1) * UNITS)
                        nc.tensor.matmul_mx(
                            out=bank[:, i * UNITS : (i + 1) * UNITS],
                            lhsT=u_codes[:, u_cols].bitcast(FP8X4),
                            lhsT_scale=u_scales[:, u_cols],
                            rhs=w_codes[:, w_cols].bitcast(FP8X4),
                            rhs_scale=w_scales[:, w_cols],
                            start=(g == 0),
                            stop=(g == PASSES - 1),
                        )
                for i in range(2):
                    t = 2 * pair + i
                    nc.vector.scalar_tensor_tensor(
                        out=v[:, block(t)],
                        in0=bank[:, i * UNITS : (i + 1) * UNITS],
                        scalar=1.0,
                        in1=plain[:, (gate * BT + t) * UNITS : (gate * BT + t + 1) * UNITS],
                        op0=ALU.mult,
                        op1=ALU.add,
                        accum_out=v_sums[:, t : t + 1],
                    )
            return v, v_sums

        def gate_cols(gate):
            return slice(gate * UNITS, (gate + 1) * UNITS)

        gates = [keep.tile([P, BT * UNITS], F32, name="gate%d" % gate) for gate in range(VECTOR_GATES)]

        def activate(gate, normed):
            if gate == 1:
                nc.scalar.activation(out=gates[gate][:], in_=normed[:], func=ACT.Sigmoid, bias=one_column[:])
            else:
                nc.scalar.activation(out=gates[gate][:], in_=normed[:], func=ACT.Sigmoid)

        def row_scale_and_bias(neg_mean, root):
            inv_std = inverse(std_plus_eps(root))
            neg_mean_over_std = small.tile([P, BT], F32, tag="neg_mean_over_std")
            nc.vector.tensor_tensor(out=neg_mean_over_std[:], in0=neg_mean[:], in1=inv_std[:], op=ALU.mult)
            return inv_std, neg_mean_over_std

        def gate_by_transposes(gate, func, v, inv_std, neg_mean_over_std, result_psum, result_tag):
            normed = work.tile([P, BT * UNITS], F32, tag="normed")
            flipped = []
            for pair in range(BT // 2):
                bank = flip_psum.tile([P, BANK], F32, tag="flip")
                for i in range(2):
                    t = 2 * pair + i
                    nc.scalar.activation(
                        out=normed[:, block(t)],
                        in_=v[:, block(t)],
                        func=ACT.Identity,
                        scale=inv_std[:, t : t + 1],
                        bias=neg_mean_over_std[:, t : t + 1],
                    )
                for c in range(GATE_CHUNKS):
                    for i in range(2):
                        t = 2 * pair + i
                        nc.tensor.transpose(
                            out=bank[:, (2 * c + i) * P : (2 * c + i + 1) * P],
                            in_=normed[:, t * UNITS + c * P : t * UNITS + (c + 1) * P],
                            identity=ident_f32[:],
                        )
                flipped.append(bank)
            gate_t = work.tile([P, BT * UNITS], F32, tag="gate_t")
            result = []
            for pair in range(BT // 2):
                for c in range(GATE_CHUNKS):
                    gamma_chunk = GAMMA_CHUNK + gate * GATE_CHUNKS + c
                    beta_chunk = BETA_CHUNK + gate * GATE_CHUNKS + c
                    nc.scalar.activation(
                        out=gate_t[:, (2 * pair + c) * UNITS : (2 * pair + c + 1) * UNITS],
                        in_=flipped[pair][:, c * UNITS : (c + 1) * UNITS],
                        func=func,
                        scale=norm_cols_f32[:, gamma_chunk : gamma_chunk + 1],
                        bias=norm_cols_f32[:, beta_chunk : beta_chunk + 1],
                    )
                bank = result_psum.tile([P, BANK], F32, tag=result_tag)
                for i in range(2):
                    for c in range(GATE_CHUNKS):
                        first = (2 * pair + c) * UNITS + i * P
                        nc.tensor.transpose(
                            out=bank[:, i * UNITS + c * P : i * UNITS + (c + 1) * P],
                            in_=gate_t[:, first : first + P],
                            identity=ident_f32[:],
                        )
                result.append(bank)
            return result

        grouped_u = [flip_u(0), flip_u(1)]
        quantise_u(0, grouped_u[0])
        plain_product(0)
        quantise_u(1, grouped_u[1])
        grouped_u = grouped_u + [flip_u(2), flip_u(3)]
        quantise_u(2, grouped_u[2])
        quantise_u(3, grouped_u[3])
        grouped_w = {0: flip_w(0, vector_helps=True)}
        quantise_w(0, 0, grouped_w[0][0])
        quantise_w(0, 1, grouped_w[0][1])
        grouped_w[1] = flip_w(1, vector_helps=False)

        vs = []
        neg_means = []
        roots = []
        centreds = []
        for gate in range(GATES - 1):
            before = gate - 1
            v, v_sums = gate_sums(gate)
            vs.append(v)
            neg_means.append(negated_mean(v_sums))
            roots.append(root_of_squares(v, neg_means[gate]))
            plain_product(gate + 1)
            quantise_w(gate + 1, 0, grouped_w[gate + 1][0])
            if before >= 0:
                std_eps = std_plus_eps(roots[before])
            quantise_w(gate + 1, 1, grouped_w[gate + 1][1])
            if before >= 0:
                inv_std = inverse(std_eps)
            if gate < VECTOR_GATES:
                centreds.append(centre(v, neg_means[gate], ln_gamma[:, gate_cols(gate)]))
            if before >= 0:
                normed = work.tile([P, BT * UNITS], F32, tag="normed")
                scale_and_shift(centreds[before], inv_std, ln_beta[:, gate_cols(before)], normed)
            if gate + 2 < GATES:
                grouped_w[gate + 2] = flip_w(gate + 2, vector_helps=False)
            if before >= 0:
                activate(before, normed)

        late = flip_psum.tile([P, 2 * BANK], BF16, tag="flip")
        spread_chunks(late[:, 0:UNITS], LNC_GAMMA_CHUNK, GATE_CHUNKS)
        spread_chunks(late[:, UNITS : 2 * UNITS], LNC_BETA_CHUNK, GATE_CHUNKS)
        lnc_gamma = late[:, 0:UNITS]
        lnc_beta = late[:, UNITS : 2 * UNITS]

        inv_std, neg_mean_over_std = row_scale_and_bias(neg_means[2], roots[2])
        v, v_sums = gate_sums(3)
        gate_g = gate_by_transposes(2, ACT.Tanh, vs[2], inv_std, neg_mean_over_std, mx_psum, "mx")
        neg_mean = negated_mean(v_sums)
        kept = keep.tile([P, BT * UNITS], F32)
        nc.vector.tensor_tensor(out=kept[:], in0=gates[1][:], in1=c_raw[:], op=ALU.mult)
        root = root_of_squares(v, neg_mean)

        fresh = keep.tile([P, BT * UNITS], F32)
        for pair in range(BT // 2):
            cols = slice(pair * BANK, (pair + 1) * BANK)
            nc.vector.tensor_tensor(out=fresh[:, cols], in0=gates[0][:, cols], in1=gate_g[pair][:], op=ALU.mult)
        cell = keep.tile([P, BT * UNITS], F32)
        cell_sums = small.tile([P, BT], F32)
        cell_neg_mean = small.tile([P, BT], F32)
        cell_sum_squares = small.tile([P, BT], F32)
        squares = work.tile([P, BT * UNITS], F32, tag="squares")
        for t in range(BT + 1):
            if t < BT:
                nc.vector.scalar_tensor_tensor(
                    out=cell[:, block(t)],
                    in0=kept[:, block(t)],
                    scalar=1.0,
                    in1=fresh[:, block(t)],
                    op0=ALU.mult,
                    op1=ALU.add,
                    accum_out=cell_sums[:, t : t + 1],
                )
            if t >= 1:
                done = slice(t - 1, t)
                nc.vector.tensor_scalar_mul(out=cell_neg_mean[:, done], in0=cell_sums[:, done], scalar1=-1.0 / UNITS)
                sum_of_squares(cell, cell_neg_mean, squares, cell_sum_squares, t - 1)
        cell_root = square_root(cell_sum_squares)

        inv_std, neg_mean_over_std = row_scale_and_bias(neg_mean, root)
        gate_o = gate_by_transposes(3, ACT.Sigmoid, v, inv_std, neg_mean_over_std, plain_psum, "plain")

        cell_centred = centre(cell, cell_neg_mean, lnc_gamma)
        new_c = keep.tile([P, BT * UNITS], F32)
        scale_and_shift(cell_centred, inverse(std_plus_eps(cell_root)), lnc_beta, new_c)
        out_0_tiles = out_0.rearrange("(p t) n -> p t n", t=BT)
        out_1_tiles = out_1.rearrange("(p t) n -> p t n", t=BT)
        for t in range(BT):
            nc.sync.dma_start(out=out_1_tiles[:, t, :], in_=new_c[:, block(t)])
        tanh_c = keep.tile([P, BT * UNITS], F32)
        new_h = keep.tile([P, BT * UNITS], F32)
        for t in range(BT):
            nc.scalar.activation(out=tanh_c[:, block(t)], in_=new_c[:, block(t)], func=ACT.Tanh)
            nc.vector.tensor_tensor(
                out=new_h[:, block(t)],
                in0=tanh_c[:, block(t)],
                in1=gate_o[t // 2][:, (t % 2) * UNITS : (t % 2 + 1) * UNITS],
                op=ALU.mult,
            )
            nc.sync.dma_start(out=out_0_tiles[:, t, :], in_=new_h[:, block(t)])
